import numpy as np
import ml_dtypes


def mxq(x, axis, fmt="e4m3"):
    dtype, down = {"e4m3": (ml_dtypes.float8_e4m3fn, 7), "e5m2": (ml_dtypes.float8_e5m2, 14)}[fmt]
    v = np.moveaxis(np.asarray(x, np.float32).astype(ml_dtypes.bfloat16).astype(np.float64), axis, -1)
    blocks = v.reshape(v.shape[:-1] + (-1, 32))
    amax = np.abs(blocks).max(-1, keepdims=True)
    byte = np.maximum(np.where(amax > 0, np.frexp(amax)[1] - 1 + 127, 0) - down, 1)
    scale = np.exp2(byte - 127.0)
    codes = (blocks / scale).astype(np.float32).astype(dtype).astype(np.float64)
    return np.moveaxis((codes * scale).reshape(v.shape), -1, axis)


WIDE = False


def mx_kscale(k):
    if not WIDE:
        return np.ones(k)
    levels = np.array([10, -10, 5, -5, 0])
    if k % 512:
        return np.exp2(np.random.permutation(np.resize(levels, k // 32))).repeat(32)
    a = np.empty((k // 512, 16))
    for p in range(k // 512):
        a[p, :8] = np.random.permutation(np.resize(levels, 8))
        for g in range(8):
            far = levels[np.abs(levels - a[p, g]) >= 10]
            a[p, g + 8] = far[np.random.randint(len(far))]
    return np.exp2(a.ravel()).repeat(32)


BF16 = ml_dtypes.bfloat16


def bf(x):
    return np.asarray(x, np.float32).astype(BF16)


def f64(x):
    return np.asarray(x).astype(np.float64)


B, T, HIDDEN, NUM_HEADS, HEAD_DIM, ROT_DIM, LATENT = 2, 512, 2048, 16, 128, 64, 512
NOPE_DIM = HEAD_DIM - ROT_DIM
BASE = 10000.0


def rope_tables():
    inv_freq = 1.0 / (BASE ** (np.arange(0, ROT_DIM, 2) / ROT_DIM))
    freqs = np.arange(T)[:, None] * inv_freq[None, :]
    emb = np.concatenate((freqs, freqs), axis=-1)
    return np.cos(emb), np.sin(emb)


def rotate_half(v):
    v1, v2 = v[..., : v.shape[-1] // 2], v[..., v.shape[-1] // 2 :]
    return np.concatenate((-v2, v1), axis=-1)


def heads(y, d):
    return y.reshape(B, T, NUM_HEADS, d).transpose(0, 2, 1, 3)


def setup_inputs():
    s, t = mx_kscale(HIDDEN), mx_kscale(LATENT)
    cos, sin = rope_tables()
    return {"x": bf(np.random.standard_normal((B, T, HIDDEN)) * s),
            "Wq_d": bf(np.random.standard_normal((HIDDEN, LATENT)) / np.sqrt(HIDDEN) / s[:, None] * t),
            "Wq_nope": bf(np.random.standard_normal((LATENT, NUM_HEADS * NOPE_DIM)) / np.sqrt(LATENT) / t[:, None]),
            "Wrq": bf(np.random.standard_normal((LATENT, NUM_HEADS * ROT_DIM)) / np.sqrt(LATENT) / t[:, None]),
            "cos": bf(cos), "sin": bf(sin)}


def reference(x, Wq_d, Wq_nope, Wrq, cos, sin):
    q_latent = mxq(f64(x), 2, "e4m3") @ mxq(f64(Wq_d), 0, "e4m3")
    lq = mxq(q_latent, 2, "e4m3")
    q_nope = heads(lq @ mxq(f64(Wq_nope), 0, "e4m3"), NOPE_DIM)
    q_rot = heads(lq @ mxq(f64(Wrq), 0, "e4m3"), ROT_DIM)
    c, sn = f64(cos)[None, None, :, :], f64(sin)[None, None, :, :]
    q_rot = q_rot * c + rotate_half(q_rot) * sn
    return np.concatenate([q_rot, q_nope], axis=-1)

@@ -1,0 +1,382 @@
+from contextlib import ExitStack
+
+import concourse.mybir as mybir
+from concourse.masks import make_identity
+
+F32 = mybir.dt.float32
+BF16 = mybir.dt.bfloat16
+U32 = mybir.dt.uint32
+U8 = mybir.dt.uint8
+FP8X4 = mybir.dt.float8_e4m3fn_x4
+MULT = mybir.AluOpType.mult
+ADD = mybir.AluOpType.add
+
+P = 128
+FLOPS = 2 * 1024 * 2048 * 512 + 2 * 1024 * 512 * 2048
+
+SCALAR_COLS = {"wd0": 176, "wd1": 176, "wd2": 176, "wd3": 176, "rq0": 176, "rq1": 176, "np0": 176, "np1": 176}
+
+def tile_multiheadlatentattention_pa_kernel(tc, x, Wq_d, Wq_nope, Wrq, cos, sin, out):
+    nc = tc.nc
+    with ExitStack() as ctx:
+        const = ctx.enter_context(tc.tile_pool(name="const", bufs=1))
+        raw = ctx.enter_context(tc.tile_pool(name="raw", bufs=1))
+        grp = ctx.enter_context(tc.tile_pool(name="grp", bufs=3))
+        mx = ctx.enter_context(tc.tile_pool(name="mx", bufs=1))
+        prod = ctx.enter_context(tc.tile_pool(name="prod", bufs=3))
+        res = ctx.enter_context(tc.tile_pool(name="res", bufs=4))
+        ps_x = ctx.enter_context(tc.psum_pool(name="ps_x", bufs=2))
+        ps_q = ctx.enter_context(tc.psum_pool(name="ps_q", bufs=1))
+        ps_r = ctx.enter_context(tc.psum_pool(name="ps_r", bufs=3))
+        ps_n = ctx.enter_context(tc.psum_pool(name="ps_n", bufs=2))
+
+
+        ident = const.tile([P, P], F32, name="ident")
+        make_identity(nc, ident[:])
+        cs = const.tile([P, 2, 256], BF16, name="cs")
+        nc.scalar.dma_start(out=cs[:, 0, :], in_=cos.rearrange("(p i) d -> p (i d)", i=4))
+        nc.scalar.dma_start(out=cs[:, 1, :], in_=sin.rearrange("(p i) d -> p (i d)", i=4))
+        ct = const.tile([P, 4, 2, 64], F32, name="ct")
+
+        tiles = {}
+        w_src = {"rq": Wrq, "np": Wq_nope}
+
+        def load(name):
+            if name[0] == "x":
+                n = int(name[1])
+                b, i = divmod(n, 4)
+                t = raw.tile([P, 2048], BF16, name="raw_" + name)
+                nc.sync.dma_start(out=t[:], in_=x[b].rearrange("(p i) k -> p i k", i=4)[:, i, :])
+            elif name[0] == "w":
+                g = int(name[2])
+                t = raw.tile([P, 4, 512], BF16, name="raw_" + name)
+                nc.sync.dma_start(out=t[:], in_=Wq_d[512 * g : 512 * (g + 1), :].rearrange("(p j) c -> p j c", j=4))
+            else:
+                t = raw.tile([P, 4, 1024], BF16, name="raw_" + name)
+                nc.sync.dma_start(out=t[:], in_=w_src[name].rearrange("(p j) n -> p j n", j=4))
+            tiles["raw_" + name] = t
+
+        def tables():
+            cv = cs[:, 0, :].rearrange("p (i d) -> p i d", d=64)
+            sv = cs[:, 1, :].rearrange("p (i d) -> p i d", d=64)
+            nc.vector.tensor_copy(out=ct[:, :, 0, :], in_=cv)
+            nc.vector.tensor_copy(out=ct[:, :, 1, 0:32], in_=sv[:, :, 32:64])
+            nc.vector.tensor_scalar_mul(out=ct[:, :, 1, 32:64], in0=sv[:, :, 0:32], scalar1=-1.0)
+
+        def get(key, pool, shape, dtype, tag):
+            if key not in tiles:
+                tiles[key] = pool.tile(shape, dtype, tag=tag, name=key, align_bytes=64)
+            return tiles[key]
+
+        def getp(key, pool, shape, tag):
+            if key not in tiles:
+                tiles[key] = pool.tile(shape, F32, tag=tag, name=key)
+            return tiles[key]
+
+        def regroup(eng, name):
+            if name[0] == "w":
+                src = tiles["raw_" + name][:].rearrange("p j (m t) -> p t m j", t=4)
+                d = get("g_" + name, grp, [P, 2048], BF16, "gw")[:].rearrange("p (t m j) -> p t m j", t=4, j=4)
+                v = P - SCALAR_COLS[name] // 4
+                if eng == "V":
+                    nc.vector.tensor_copy(out=d[:, :, 0:v, :], in_=src[:, :, 0:v, :])
+                else:
+                    nc.scalar.copy(out=d[:, :, v:P, :], in_=src[:, :, v:P, :])
+                return
+            else:
+                hg = int(name[2])
+                src = tiles["raw_" + name[0:2]][:, :, 512 * hg : 512 * (hg + 1)]
+            v = 512 - SCALAR_COLS[name]
+            d = get("g_" + name, grp, [P, 2048], BF16, "gw")[:].rearrange("p (c t) -> p c t", t=4)
+            if eng == "V":
+                nc.vector.tensor_copy(
+                    out=d[:, 0:v, :].rearrange("p (c i) t -> p c t i", i=4),
+                    in_=src[:, :, 0:v].rearrange("p t (c i) -> p c t i", i=4),
+                )
+            else:
+                nc.scalar.copy(
+                    out=d[:, v:512, :].rearrange("p (c i) t -> p c t i", i=4),
+                    in_=src[:, :, v:512].rearrange("p t (c i) -> p c t i", i=4),
+                )
+
+        def quantise(name, words):
+            codes = mx.tile([P, words], U32, name="c_" + name, align_bytes=64)
+            scales = mx.tile([P, words], U8, name="s_" + name, align_bytes=64)
+            nc.vector.quantize_mx(out=codes[:].bitcast(FP8X4), scales=scales[:], in_=tiles["g_" + name][:])
+            tiles["c_" + name] = codes
+            tiles["s_" + name] = scales
+
+        def x_t(n, hb):
+            xw = tiles["raw_x%d" % n][:].bitcast(F32)
+            xt = getp("xt%d_%d" % (n, hb), ps_x, [P, 4, P], "xt")
+            for w in range(4):
+                c0 = 256 * (2 * hb + w // 2)
+                nc.tensor.transpose(xt[:, w, :], xw[:, c0 + w % 2 : c0 + 256 : 2], ident[:])
+
+        def x_c(n, hb):
+            gx = get("g_x%d" % n, grp, [P, 2048], BF16, "gx")
+            gxw = gx[:].bitcast(F32).rearrange("q (g p u) -> q g p u", g=4, u=2)
+            nc.scalar.copy(
+                out=gxw[:, 2 * hb : 2 * hb + 2],
+                in_=tiles["xt%d_%d" % (n, hb)][:].rearrange("q (g u) p -> q g p u", u=2),
+            )
+
+        def s1(n):
+            qp = getp("qp%d" % n, ps_q, [P, 4, P], "qp")
+            for j in range(4):
+                for g in range(4):
+                    nc.tensor.matmul_mx(
+                        out=qp[:, j, :],
+                        lhsT=tiles["c_wd%d" % g][:, P * j : P * (j + 1)].bitcast(FP8X4),
+                        lhsT_scale=tiles["s_wd%d" % g][:, P * j : P * (j + 1)],
+                        rhs=tiles["c_x%d" % n][:, P * g : P * (g + 1)].bitcast(FP8X4),
+                        rhs_scale=tiles["s_x%d" % n][:, P * g : P * (g + 1)],
+                        start=(g == 0),
+                        stop=(g == 3),
+                    )
+
+        def q_c(n):
+            gq = get("g_q%d" % n, grp, [P, 512], BF16, "gq")
+            nc.scalar.copy(
+                out=gq[:].rearrange("p (n j) -> p n j", j=4),
+                in_=tiles["qp%d" % n][:].rearrange("p j n -> p n j"),
+            )
+
+        def s2(kind, pool, n, hg):
+            acc = getp("%s%d_%d" % (kind, n, hg), pool, [P, 512], kind)
+            nc.tensor.matmul_mx(
+                out=acc[:],
+                lhsT=tiles["c_q%d" % n][:].bitcast(FP8X4),
+                lhsT_scale=tiles["s_q%d" % n][:],
+                rhs=tiles["c_%s%d" % (kind, hg)][:].bitcast(FP8X4),
+                rhs_scale=tiles["s_%s%d" % (kind, hg)][:],
+                start=True,
+                stop=True,
+            )
+
+        def r_v(n, hg):
+            a = get("ab%d_%d" % (n // 2, hg), prod, [P, 2, 2, 512], F32, "ab")
+            nc.vector.tensor_tensor(
+                out=a[:, n % 2].rearrange("p a (h d) -> p a h d", d=64),
+                in0=tiles["rq%d_%d" % (n, hg)][:].rearrange("p (h d) -> p h d", d=64).unsqueeze(1).to_broadcast([P, 2, 8, 64]),
+                in1=ct[:, n % 4].unsqueeze(2).to_broadcast([P, 2, 8, 64]),
+                op=MULT,
+            )
+
+        def n_c(n, hg):
+            o = get("ot%d_%d" % (n // 2, hg), res, [P, 8, 2, P], F32, "ot")
+            nc.scalar.copy(
+                out=o[:, :, n % 2, 64:128],
+                in_=tiles["np%d_%d" % (n, hg)][:].rearrange("p (h d) -> p h d", d=64),
+            )
+
+        def add(eng, s, hg, half):
+            o = get("ot%d_%d" % (s, hg), res, [P, 8, 2, P], F32, "ot")
+            a = tiles["ab%d_%d" % (s, hg)]
+            lo = 32 * half
+            sw = 32 * (1 - half)
+            eng.tensor_tensor(
+                out=o[:, :, :, lo : lo + 32].rearrange("p h s d -> p s h d"),
+                in0=a[:, :, 0].rearrange("p s (h d) -> p s h d", d=64)[:, :, :, lo : lo + 32],
+                in1=a[:, :, 1].rearrange("p s (h d) -> p s h d", d=64)[:, :, :, sw : sw + 32],
+                op=ADD,
+            )
+
+        def store(s, hg):
+            b, ip = divmod(s, 2)
+            nc.sync.dma_start(
+                out=out[b, 8 * hg : 8 * hg + 8].rearrange("h (p i) d -> p h (i d)", i=4)[:, :, 256 * ip : 256 * (ip + 1)],
+                in_=tiles["ot%d_%d" % (s, hg)][:].rearrange("p h s d -> p h (s d)"),
+            )
+
+        load("x0")
+        load("wd0")
+        load("wd1")
+        load("wd2")
+        load("wd3")
+        load("x1")
+        load("rq")
+        load("np")
+        load("x2")
+        load("x3")
+        load("x4")
+        load("x5")
+        load("x6")
+        load("x7")
+        tables()
+        x_t(0, 0)
+        x_t(0, 1)
+        x_c(0, 0)
+        x_c(0, 1)
+        regroup("V", "wd0")
+        regroup("S", "wd0")
+        quantise("x0", 512)
+        regroup("V", "wd1")
+        regroup("S", "wd1")
+        quantise("wd0", 512)
+        regroup("V", "wd2")
+        regroup("S", "wd2")
+        quantise("wd1", 512)
+        regroup("V", "wd3")
+        regroup("S", "wd3")
+        quantise("wd2", 512)
+        x_t(1, 0)
+        x_t(1, 1)
+        x_c(1, 0)
+        x_c(1, 1)
+        quantise("wd3", 512)
+        s1(0)
+        quantise("x1", 512)
+        regroup("V", "rq0")
+        regroup("S", "rq0")
+        quantise("rq0", 512)
+        regroup("V", "rq1")
+        regroup("S", "rq1")
+        q_c(0)
+        s1(1)
+        quantise("q0", P)
+        quantise("rq1", 512)
+        s2("rq", ps_r, 0, 0)
+        s2("rq", ps_r, 0, 1)
+        x_t(2, 0)
+        x_t(2, 1)
+        r_v(0, 0)
+        q_c(1)
+        x_c(2, 0)
+        x_c(2, 1)
+        x_t(3, 0)
+        x_t(3, 1)
+        regroup("V", "np0")
+        regroup("S", "np0")
+        quantise("q1", P)
+        s2("rq", ps_r, 1, 0)
+        s2("rq", ps_r, 1, 1)
+        quantise("x2", 512)
+        s1(2)
+        r_v(0, 1)
+        quantise("np0", 512)
+        regroup("V", "np1")
+        regroup("S", "np1")
+        x_c(3, 0)
+        x_c(3, 1)
+        q_c(2)
+        quantise("x3", 512)
+        quantise("np1", 512)
+        x_t(4, 0)
+        x_t(4, 1)
+        s2("np", ps_n, 0, 0)
+        s2("np", ps_n, 0, 1)
+        s1(3)
+        r_v(1, 0)
+        n_c(0, 0)
+        x_c(4, 0)
+        x_c(4, 1)
+        quantise("q2", P)
+        s2("rq", ps_r, 2, 0)
+        s2("rq", ps_r, 2, 1)
+        r_v(1, 1)
+        n_c(0, 1)
+        q_c(3)
+        quantise("x4", 512)
+        x_t(5, 0)
+        x_t(5, 1)
+        s2("np", ps_n, 1, 0)
+        s2("np", ps_n, 1, 1)
+        add(nc.gpsimd, 0, 0, 0)
+        add(nc.gpsimd, 0, 0, 1)
+        add(nc.gpsimd, 0, 1, 0)
+        add(nc.gpsimd, 0, 1, 1)
+        s1(4)
+        r_v(2, 0)
+        n_c(1, 0)
+        x_c(5, 0)
+        x_c(5, 1)
+        quantise("q3", P)
+        s2("rq", ps_r, 3, 0)
+        s2("rq", ps_r, 3, 1)
+        r_v(2, 1)
+        n_c(1, 1)
+        q_c(4)
+        quantise("x5", 512)
+        x_t(6, 0)
+        x_t(6, 1)
+        s2("np", ps_n, 2, 0)
+        s2("np", ps_n, 2, 1)
+        store(0, 0)
+        store(0, 1)
+        s1(5)
+        r_v(3, 0)
+        n_c(2, 0)
+        x_c(6, 0)
+        x_c(6, 1)
+        quantise("q4", P)
+        s2("rq", ps_r, 4, 0)
+        s2("rq", ps_r, 4, 1)
+        r_v(3, 1)
+        n_c(2, 1)
+        q_c(5)
+        quantise("x6", 512)
+        x_t(7, 0)
+        x_t(7, 1)
+        s2("np", ps_n, 3, 0)
+        s2("np", ps_n, 3, 1)
+        add(nc.gpsimd, 1, 0, 0)
+        add(nc.gpsimd, 1, 0, 1)
+        add(nc.gpsimd, 1, 1, 0)
+        add(nc.gpsimd, 1, 1, 1)
+        s1(6)
+        r_v(4, 0)
+        n_c(3, 0)
+        x_c(7, 0)
+        x_c(7, 1)
+        quantise("q5", P)
+        s2("rq", ps_r, 5, 0)
+        s2("rq", ps_r, 5, 1)
+        r_v(4, 1)
+        n_c(3, 1)
+        q_c(6)
+        quantise("x7", 512)
+        s2("np", ps_n, 4, 0)
+        s2("np", ps_n, 4, 1)
+        store(1, 0)
+        store(1, 1)
+        s1(7)
+        r_v(5, 0)
+        n_c(4, 0)
+        quantise("q6", P)
+        s2("rq", ps_r, 6, 0)
+        s2("rq", ps_r, 6, 1)
+        r_v(5, 1)
+        n_c(4, 1)
+        q_c(7)
+        s2("np", ps_n, 5, 0)
+        s2("np", ps_n, 5, 1)
+        add(nc.gpsimd, 2, 0, 0)
+        add(nc.gpsimd, 2, 0, 1)
+        add(nc.gpsimd, 2, 1, 0)
+        add(nc.gpsimd, 2, 1, 1)
+        r_v(6, 0)
+        n_c(5, 0)
+        quantise("q7", P)
+        s2("rq", ps_r, 7, 0)
+        s2("rq", ps_r, 7, 1)
+        r_v(6, 1)
+        n_c(5, 1)
+        s2("np", ps_n, 6, 0)
+        s2("np", ps_n, 6, 1)
+        store(2, 0)
+        store(2, 1)
+        r_v(7, 0)
+        n_c(6, 0)
+        r_v(7, 1)
+        n_c(6, 1)
+        s2("np", ps_n, 7, 0)
+        s2("np", ps_n, 7, 1)
+        add(nc.gpsimd, 3, 0, 0)
+        add(nc.gpsimd, 3, 0, 1)
+        add(nc.vector, 3, 1, 0)
+        add(nc.vector, 3, 1, 1)
+        n_c(7, 0)
+        n_c(7, 1)
+        store(3, 0)
+        store(3, 1)

@@ -79,9 +79,15 @@ def tile_multiheadlatentattention_pa_kernel(tc, x, Wq_d, Wq_nope, Wrq, cos, sin,
                 d = get("g_" + name, grp, [P, 2048], BF16, "gw")[:].rearrange("p (t m j) -> p t m j", t=4, j=4)
                 v = P - SCALAR_COLS[name] // 4
                 if eng == "V":
-                    nc.vector.tensor_copy(out=d[:, :, 0:v, :], in_=src[:, :, 0:v, :])
+                    nc.vector.tensor_copy(
+                        out=d[:, :, 0:v, :].rearrange("p t m j -> p m j t"),
+                        in_=src[:, :, 0:v, :].rearrange("p t m j -> p m j t"),
+                    )
                 else:
-                    nc.scalar.copy(out=d[:, :, v:P, :], in_=src[:, :, v:P, :])
+                    nc.scalar.copy(
+                        out=d[:, :, v:P, :].rearrange("p t m j -> p m j t"),
+                        in_=src[:, :, v:P, :].rearrange("p t m j -> p m j t"),
+                    )
                 return
             else:
                 hg = int(name[2])

@@ -80,8 +80,8 @@ def tile_multiheadlatentattention_pa_kernel(tc, x, Wq_d, Wq_nope, Wrq, cos, sin,
                 v = P - SCALAR_COLS[name] // 4
                 if eng == "V":
                     nc.vector.tensor_copy(
-                        out=d[:, :, 0:v, :].rearrange("p t m j -> p m j t"),
-                        in_=src[:, :, 0:v, :].rearrange("p t m j -> p m j t"),
+                        out=d[:, :, 0:v, :].rearrange("p t (m e) j -> p m j e t", e=2),
+                        in_=src[:, :, 0:v, :].rearrange("p t (m e) j -> p m j e t", e=2),
                     )
                 else:
                     nc.scalar.copy(
@@ -96,13 +96,13 @@ def tile_multiheadlatentattention_pa_kernel(tc, x, Wq_d, Wq_nope, Wrq, cos, sin,
             d = get("g_" + name, grp, [P, 2048], BF16, "gw")[:].rearrange("p (c t) -> p c t", t=4)
             if eng == "V":
                 nc.vector.tensor_copy(
-                    out=d[:, 0:v, :].rearrange("p (c i) t -> p c t i", i=4),
-                    in_=src[:, :, 0:v].rearrange("p t (c i) -> p c t i", i=4),
+                    out=d[:, 0:v, :].rearrange("p (c i) t -> p c t i", i=8),
+                    in_=src[:, :, 0:v].rearrange("p t (c i) -> p c t i", i=8),
                 )
             else:
                 nc.scalar.copy(
-                    out=d[:, v:512, :].rearrange("p (c i) t -> p c t i", i=4),
-                    in_=src[:, :, v:512].rearrange("p t (c i) -> p c t i", i=4),
+                    out=d[:, v:512, :].rearrange("p (c i) t -> p c t i", i=8),
+                    in_=src[:, :, v:512].rearrange("p t (c i) -> p c t i", i=8),
                 )
 
         def quantise(name, words):

@@ -14,7 +14,7 @@ ADD = mybir.AluOpType.add
 P = 128
 FLOPS = 2 * 1024 * 2048 * 512 + 2 * 1024 * 512 * 2048
 
-SCALAR_COLS = {"wd0": 176, "wd1": 176, "wd2": 176, "wd3": 176, "rq0": 176, "rq1": 176, "np0": 176, "np1": 176}
+SCALAR_COLS = {"wd": 176, "rq": 176, "np": 176}
 
 def tile_multiheadlatentattention_pa_kernel(tc, x, Wq_d, Wq_nope, Wrq, cos, sin, out):
     nc = tc.nc
@@ -24,7 +24,7 @@ def tile_multiheadlatentattention_pa_kernel(tc, x, Wq_d, Wq_nope, Wrq, cos, sin,
         grp = ctx.enter_context(tc.tile_pool(name="grp", bufs=3))
         mx = ctx.enter_context(tc.tile_pool(name="mx", bufs=1))
         prod = ctx.enter_context(tc.tile_pool(name="prod", bufs=3))
-        res = ctx.enter_context(tc.tile_pool(name="res", bufs=4))
+        res = ctx.enter_context(tc.tile_pool(name="res", bufs=6))
         ps_x = ctx.enter_context(tc.psum_pool(name="ps_x", bufs=2))
         ps_q = ctx.enter_context(tc.psum_pool(name="ps_q", bufs=1))
         ps_r = ctx.enter_context(tc.psum_pool(name="ps_r", bufs=3))
@@ -59,9 +59,9 @@ def tile_multiheadlatentattention_pa_kernel(tc, x, Wq_d, Wq_nope, Wrq, cos, sin,
         def tables():
             cv = cs[:, 0, :].rearrange("p (i d) -> p i d", d=64)
             sv = cs[:, 1, :].rearrange("p (i d) -> p i d", d=64)
-            nc.vector.tensor_copy(out=ct[:, :, 0, :], in_=cv)
-            nc.vector.tensor_copy(out=ct[:, :, 1, 0:32], in_=sv[:, :, 32:64])
-            nc.vector.tensor_scalar_mul(out=ct[:, :, 1, 32:64], in0=sv[:, :, 0:32], scalar1=-1.0)
+            nc.scalar.copy(out=ct[:, :, 0, :], in_=cv)
+            nc.scalar.copy(out=ct[:, :, 1, 0:32], in_=sv[:, :, 32:64])
+            nc.scalar.mul(out=ct[:, :, 1, 32:64], in_=sv[:, :, 0:32], mul=-1.0)
 
         def get(key, pool, shape, dtype, tag):
             if key not in tiles:
@@ -77,11 +77,11 @@ def tile_multiheadlatentattention_pa_kernel(tc, x, Wq_d, Wq_nope, Wrq, cos, sin,
             if name[0] == "w":
                 src = tiles["raw_" + name][:].rearrange("p j (m t) -> p t m j", t=4)
                 d = get("g_" + name, grp, [P, 2048], BF16, "gw")[:].rearrange("p (t m j) -> p t m j", t=4, j=4)
-                v = P - SCALAR_COLS[name] // 4
+                v = P - SCALAR_COLS[name[0:2]] // 4
                 if eng == "V":
                     nc.vector.tensor_copy(
-                        out=d[:, :, 0:v, :].rearrange("p t (m e) j -> p m j e t", e=2),
-                        in_=src[:, :, 0:v, :].rearrange("p t (m e) j -> p m j e t", e=2),
+                        out=d[:, :, 0:v, :].rearrange("p t m j -> p m j t"),
+                        in_=src[:, :, 0:v, :].rearrange("p t m j -> p m j t"),
                     )
                 else:
                     nc.scalar.copy(
@@ -92,7 +92,7 @@ def tile_multiheadlatentattention_pa_kernel(tc, x, Wq_d, Wq_nope, Wrq, cos, sin,
             else:
                 hg = int(name[2])
                 src = tiles["raw_" + name[0:2]][:, :, 512 * hg : 512 * (hg + 1)]
-            v = 512 - SCALAR_COLS[name]
+            v = 512 - SCALAR_COLS[name[0:2]]
             d = get("g_" + name, grp, [P, 2048], BF16, "gw")[:].rearrange("p (c t) -> p c t", t=4)
             if eng == "V":
                 nc.vector.tensor_copy(
@@ -201,10 +201,10 @@ def tile_multiheadlatentattention_pa_kernel(tc, x, Wq_d, Wq_nope, Wrq, cos, sin,
         load("wd2")
         load("wd3")
         load("x1")
-        load("rq")
-        load("np")
         load("x2")
+        load("rq")
         load("x3")
+        load("np")
         load("x4")
         load("x5")
         load("x6")
@@ -233,155 +233,155 @@ def tile_multiheadlatentattention_pa_kernel(tc, x, Wq_d, Wq_nope, Wrq, cos, sin,
         quantise("wd3", 512)
         s1(0)
         quantise("x1", 512)
+        x_t(2, 0)
+        x_t(2, 1)
+        q_c(0)
+        x_c(2, 0)
+        x_c(2, 1)
+        s1(1)
         regroup("V", "rq0")
         regroup("S", "rq0")
-        quantise("rq0", 512)
+        quantise("q0", P)
+        quantise("x2", 512)
+        x_t(3, 0)
+        x_t(3, 1)
+        q_c(1)
         regroup("V", "rq1")
         regroup("S", "rq1")
-        q_c(0)
-        s1(1)
-        quantise("q0", P)
+        quantise("rq0", 512)
+        x_c(3, 0)
+        x_c(3, 1)
+        s1(2)
+        regroup("V", "np0")
+        regroup("S", "np0")
         quantise("rq1", 512)
         s2("rq", ps_r, 0, 0)
         s2("rq", ps_r, 0, 1)
-        x_t(2, 0)
-        x_t(2, 1)
+        quantise("x3", 512)
+        q_c(2)
+        regroup("V", "np1")
+        regroup("S", "np1")
+        quantise("np0", 512)
+        x_t(4, 0)
+        x_t(4, 1)
+        quantise("np1", 512)
         r_v(0, 0)
-        q_c(1)
-        x_c(2, 0)
-        x_c(2, 1)
-        x_t(3, 0)
-        x_t(3, 1)
-        regroup("V", "np0")
-        regroup("S", "np0")
+        s1(3)
+        x_c(4, 0)
+        x_c(4, 1)
         quantise("q1", P)
         s2("rq", ps_r, 1, 0)
         s2("rq", ps_r, 1, 1)
-        quantise("x2", 512)
-        s1(2)
         r_v(0, 1)
-        quantise("np0", 512)
-        regroup("V", "np1")
-        regroup("S", "np1")
-        x_c(3, 0)
-        x_c(3, 1)
-        q_c(2)
-        quantise("x3", 512)
-        quantise("np1", 512)
-        x_t(4, 0)
-        x_t(4, 1)
+        q_c(3)
+        quantise("x4", 512)
         s2("np", ps_n, 0, 0)
         s2("np", ps_n, 0, 1)
-        s1(3)
+        x_t(5, 0)
+        x_t(5, 1)
         r_v(1, 0)
+        s1(4)
         n_c(0, 0)
-        x_c(4, 0)
-        x_c(4, 1)
+        n_c(0, 1)
+        x_c(5, 0)
+        x_c(5, 1)
         quantise("q2", P)
         s2("rq", ps_r, 2, 0)
         s2("rq", ps_r, 2, 1)
         r_v(1, 1)
-        n_c(0, 1)
-        q_c(3)
-        quantise("x4", 512)
-        x_t(5, 0)
-        x_t(5, 1)
-        s2("np", ps_n, 1, 0)
-        s2("np", ps_n, 1, 1)
         add(nc.gpsimd, 0, 0, 0)
         add(nc.gpsimd, 0, 0, 1)
         add(nc.gpsimd, 0, 1, 0)
         add(nc.gpsimd, 0, 1, 1)
-        s1(4)
+        q_c(4)
+        quantise("x5", 512)
+        s2("np", ps_n, 1, 0)
+        s2("np", ps_n, 1, 1)
+        x_t(6, 0)
+        x_t(6, 1)
         r_v(2, 0)
+        s1(5)
         n_c(1, 0)
-        x_c(5, 0)
-        x_c(5, 1)
+        n_c(1, 1)
+        store(0, 0)
+        store(0, 1)
+        x_c(6, 0)
+        x_c(6, 1)
         quantise("q3", P)
         s2("rq", ps_r, 3, 0)
         s2("rq", ps_r, 3, 1)
         r_v(2, 1)
-        n_c(1, 1)
-        q_c(4)
-        quantise("x5", 512)
-        x_t(6, 0)
-        x_t(6, 1)
+        q_c(5)
+        quantise("x6", 512)
         s2("np", ps_n, 2, 0)
         s2("np", ps_n, 2, 1)
-        store(0, 0)
-        store(0, 1)
-        s1(5)
+        x_t(7, 0)
+        x_t(7, 1)
         r_v(3, 0)
+        s1(6)
         n_c(2, 0)
-        x_c(6, 0)
-        x_c(6, 1)
+        n_c(2, 1)
+        x_c(7, 0)
+        x_c(7, 1)
         quantise("q4", P)
         s2("rq", ps_r, 4, 0)
         s2("rq", ps_r, 4, 1)
         r_v(3, 1)
-        n_c(2, 1)
-        q_c(5)
-        quantise("x6", 512)
-        x_t(7, 0)
-        x_t(7, 1)
-        s2("np", ps_n, 3, 0)
-        s2("np", ps_n, 3, 1)
         add(nc.gpsimd, 1, 0, 0)
         add(nc.gpsimd, 1, 0, 1)
         add(nc.gpsimd, 1, 1, 0)
         add(nc.gpsimd, 1, 1, 1)
-        s1(6)
+        q_c(6)
+        quantise("x7", 512)
+        s2("np", ps_n, 3, 0)
+        s2("np", ps_n, 3, 1)
         r_v(4, 0)
+        s1(7)
         n_c(3, 0)
-        x_c(7, 0)
-        x_c(7, 1)
+        n_c(3, 1)
+        store(1, 0)
+        store(1, 1)
         quantise("q5", P)
         s2("rq", ps_r, 5, 0)
         s2("rq", ps_r, 5, 1)
         r_v(4, 1)
-        n_c(3, 1)
-        q_c(6)
-        quantise("x7", 512)
+        q_c(7)
         s2("np", ps_n, 4, 0)
         s2("np", ps_n, 4, 1)
-        store(1, 0)
-        store(1, 1)
-        s1(7)
         r_v(5, 0)
         n_c(4, 0)
+        n_c(4, 1)
         quantise("q6", P)
         s2("rq", ps_r, 6, 0)
         s2("rq", ps_r, 6, 1)
         r_v(5, 1)
-        n_c(4, 1)
-        q_c(7)
-        s2("np", ps_n, 5, 0)
-        s2("np", ps_n, 5, 1)
         add(nc.gpsimd, 2, 0, 0)
         add(nc.gpsimd, 2, 0, 1)
         add(nc.gpsimd, 2, 1, 0)
         add(nc.gpsimd, 2, 1, 1)
+        s2("np", ps_n, 5, 0)
+        s2("np", ps_n, 5, 1)
         r_v(6, 0)
         n_c(5, 0)
+        n_c(5, 1)
+        store(2, 0)
+        store(2, 1)
         quantise("q7", P)
         s2("rq", ps_r, 7, 0)
         s2("rq", ps_r, 7, 1)
         r_v(6, 1)
-        n_c(5, 1)
         s2("np", ps_n, 6, 0)
         s2("np", ps_n, 6, 1)
-        store(2, 0)
-        store(2, 1)
         r_v(7, 0)
         n_c(6, 0)
-        r_v(7, 1)
         n_c(6, 1)
-        s2("np", ps_n, 7, 0)
-        s2("np", ps_n, 7, 1)
-        add(nc.gpsimd, 3, 0, 0)
-        add(nc.gpsimd, 3, 0, 1)
+        r_v(7, 1)
+        add(nc.vector, 3, 0, 0)
+        add(nc.vector, 3, 0, 1)
         add(nc.vector, 3, 1, 0)
         add(nc.vector, 3, 1, 1)
+        s2("np", ps_n, 7, 0)
+        s2("np", ps_n, 7, 1)
         n_c(7, 0)
         n_c(7, 1)
         store(3, 0)

@@ -52,8 +52,9 @@ def tile_multiheadlatentattention_pa_kernel(tc, x, Wq_d, Wq_nope, Wrq, cos, sin,
                 t = raw.tile([P, 4, 512], BF16, name="raw_" + name)
                 nc.sync.dma_start(out=t[:], in_=Wq_d[512 * g : 512 * (g + 1), :].rearrange("(p j) c -> p j c", j=4))
             else:
-                t = raw.tile([P, 4, 1024], BF16, name="raw_" + name)
-                nc.sync.dma_start(out=t[:], in_=w_src[name].rearrange("(p j) n -> p j n", j=4))
+                hg = int(name[2])
+                t = raw.tile([P, 4, 512], BF16, name="raw_" + name)
+                nc.sync.dma_start(out=t[:], in_=w_src[name[0:2]].rearrange("(p j) n -> p j n", j=4)[:, :, 512 * hg : 512 * (hg + 1)])
             tiles["raw_" + name] = t
 
         def tables():
@@ -91,7 +92,7 @@ def tile_multiheadlatentattention_pa_kernel(tc, x, Wq_d, Wq_nope, Wrq, cos, sin,
                 return
             else:
                 hg = int(name[2])
-                src = tiles["raw_" + name[0:2]][:, :, 512 * hg : 512 * (hg + 1)]
+                src = tiles["raw_" + name][:]
             v = 512 - SCALAR_COLS[name[0:2]]
             d = get("g_" + name, grp, [P, 2048], BF16, "gw")[:].rearrange("p (c t) -> p c t", t=4)
             if eng == "V":
@@ -201,10 +202,12 @@ def tile_multiheadlatentattention_pa_kernel(tc, x, Wq_d, Wq_nope, Wrq, cos, sin,
         load("wd2")
         load("wd3")
         load("x1")
+        load("rq0")
         load("x2")
-        load("rq")
+        load("rq1")
         load("x3")
-        load("np")
+        load("np0")
+        load("np1")
         load("x4")
         load("x5")
         load("x6")
@@ -233,30 +236,30 @@ def tile_multiheadlatentattention_pa_kernel(tc, x, Wq_d, Wq_nope, Wrq, cos, sin,
         quantise("wd3", 512)
         s1(0)
         quantise("x1", 512)
+        regroup("V", "rq0")
+        regroup("S", "rq0")
         x_t(2, 0)
         x_t(2, 1)
         q_c(0)
         x_c(2, 0)
         x_c(2, 1)
         s1(1)
-        regroup("V", "rq0")
-        regroup("S", "rq0")
         quantise("q0", P)
+        regroup("V", "rq1")
+        regroup("S", "rq1")
+        quantise("rq0", 512)
         quantise("x2", 512)
         x_t(3, 0)
         x_t(3, 1)
         q_c(1)
-        regroup("V", "rq1")
-        regroup("S", "rq1")
-        quantise("rq0", 512)
         x_c(3, 0)
         x_c(3, 1)
-        s1(2)
-        regroup("V", "np0")
-        regroup("S", "np0")
         quantise("rq1", 512)
+        s1(2)
         s2("rq", ps_r, 0, 0)
         s2("rq", ps_r, 0, 1)
+        regroup("V", "np0")
+        regroup("S", "np0")
         quantise("x3", 512)
         q_c(2)
         regroup("V", "np1")

from contextlib import ExitStack

import concourse.mybir as mybir
from concourse.masks import make_identity

F32 = mybir.dt.float32
BF16 = mybir.dt.bfloat16
U32 = mybir.dt.uint32
U8 = mybir.dt.uint8
FP8X4 = mybir.dt.float8_e4m3fn_x4
MULT = mybir.AluOpType.mult
ADD = mybir.AluOpType.add

P = 128
FLOPS = 2 * 1024 * 2048 * 512 + 2 * 1024 * 512 * 2048

SCALAR_COLS = {"wd": 176, "rq": 176, "np": 176}

def tile_multiheadlatentattention_pa_kernel(tc, x, Wq_d, Wq_nope, Wrq, cos, sin, out):
    nc = tc.nc
    with ExitStack() as ctx:
        const = ctx.enter_context(tc.tile_pool(name="const", bufs=1))
        raw = ctx.enter_context(tc.tile_pool(name="raw", bufs=1))
        grp = ctx.enter_context(tc.tile_pool(name="grp", bufs=3))
        mx = ctx.enter_context(tc.tile_pool(name="mx", bufs=1))
        prod = ctx.enter_context(tc.tile_pool(name="prod", bufs=3))
        res = ctx.enter_context(tc.tile_pool(name="res", bufs=6))
        ps_x = ctx.enter_context(tc.psum_pool(name="ps_x", bufs=2))
        ps_q = ctx.enter_context(tc.psum_pool(name="ps_q", bufs=1))
        ps_r = ctx.enter_context(tc.psum_pool(name="ps_r", bufs=3))
        ps_n = ctx.enter_context(tc.psum_pool(name="ps_n", bufs=2))


        ident = const.tile([P, P], F32, name="ident")
        make_identity(nc, ident[:])
        cs = const.tile([P, 2, 256], BF16, name="cs")
        nc.scalar.dma_start(out=cs[:, 0, :], in_=cos.rearrange("(p i) d -> p (i d)", i=4))
        nc.scalar.dma_start(out=cs[:, 1, :], in_=sin.rearrange("(p i) d -> p (i d)", i=4))
        ct = const.tile([P, 4, 2, 64], F32, name="ct")

        tiles = {}
        w_src = {"rq": Wrq, "np": Wq_nope}

        def load(name):
            if name[0] == "x":
                n = int(name[1])
                b, i = divmod(n, 4)
                t = raw.tile([P, 2048], BF16, name="raw_" + name)
                nc.sync.dma_start(out=t[:], in_=x[b].rearrange("(p i) k -> p i k", i=4)[:, i, :])
            elif name[0] == "w":
                g = int(name[2])
                t = raw.tile([P, 4, 512], BF16, name="raw_" + name)
                nc.sync.dma_start(out=t[:], in_=Wq_d[512 * g : 512 * (g + 1), :].rearrange("(p j) c -> p j c", j=4))
            else:
                hg = int(name[2])
                t = raw.tile([P, 4, 512], BF16, name="raw_" + name)
                nc.sync.dma_start(out=t[:], in_=w_src[name[0:2]].rearrange("(p j) n -> p j n", j=4)[:, :, 512 * hg : 512 * (hg + 1)])
            tiles["raw_" + name] = t

        def tables():
            cv = cs[:, 0, :].rearrange("p (i d) -> p i d", d=64)
            sv = cs[:, 1, :].rearrange("p (i d) -> p i d", d=64)
            nc.scalar.copy(out=ct[:, :, 0, :], in_=cv)
            nc.scalar.copy(out=ct[:, :, 1, 0:32], in_=sv[:, :, 32:64])
            nc.scalar.mul(out=ct[:, :, 1, 32:64], in_=sv[:, :, 0:32], mul=-1.0)

        def get(key, pool, shape, dtype, tag):
            if key not in tiles:
                tiles[key] = pool.tile(shape, dtype, tag=tag, name=key, align_bytes=64)
            return tiles[key]

        def getp(key, pool, shape, tag):
            if key not in tiles:
                tiles[key] = pool.tile(shape, F32, tag=tag, name=key)
            return tiles[key]

        def regroup(eng, name):
            if name[0] == "w":
                src = tiles["raw_" + name][:].rearrange("p j (m t) -> p t m j", t=4)
                d = get("g_" + name, grp, [P, 2048], BF16, "gw")[:].rearrange("p (t m j) -> p t m j", t=4, j=4)
                v = P - SCALAR_COLS[name[0:2]] // 4
                if eng == "V":
                    nc.vector.tensor_copy(
                        out=d[:, :, 0:v, :].rearrange("p t m j -> p m j t"),
                        in_=src[:, :, 0:v, :].rearrange("p t m j -> p m j t"),
                    )
                else:
                    nc.scalar.copy(
                        out=d[:, :, v:P, :].rearrange("p t m j -> p m j t"),
                        in_=src[:, :, v:P, :].rearrange("p t m j -> p m j t"),
                    )
                return
            else:
                hg = int(name[2])
                src = tiles["raw_" + name][:]
            v = 512 - SCALAR_COLS[name[0:2]]
            d = get("g_" + name, grp, [P, 2048], BF16, "gw")[:].rearrange("p (c t) -> p c t", t=4)
            if eng == "V":
                nc.vector.tensor_copy(
                    out=d[:, 0:v, :].rearrange("p (c i) t -> p c t i", i=8),
                    in_=src[:, :, 0:v].rearrange("p t (c i) -> p c t i", i=8),
                )
            else:
                nc.scalar.copy(
                    out=d[:, v:512, :].rearrange("p (c i) t -> p c t i", i=8),
                    in_=src[:, :, v:512].rearrange("p t (c i) -> p c t i", i=8),
                )

        def quantise(name, words):
            codes = mx.tile([P, words], U32, name="c_" + name, align_bytes=64)
            scales = mx.tile([P, words], U8, name="s_" + name, align_bytes=64)
            nc.vector.quantize_mx(out=codes[:].bitcast(FP8X4), scales=scales[:], in_=tiles["g_" + name][:])
            tiles["c_" + name] = codes
            tiles["s_" + name] = scales

        def x_t(n, hb):
            xw = tiles["raw_x%d" % n][:].bitcast(F32)
            xt = getp("xt%d_%d" % (n, hb), ps_x, [P, 4, P], "xt")
            for w in range(4):
                c0 = 256 * (2 * hb + w // 2)
                nc.tensor.transpose(xt[:, w, :], xw[:, c0 + w % 2 : c0 + 256 : 2], ident[:])

        def x_c(n, hb):
            gx = get("g_x%d" % n, grp, [P, 2048], BF16, "gx")
            gxw = gx[:].bitcast(F32).rearrange("q (g p u) -> q g p u", g=4, u=2)
            nc.scalar.copy(
                out=gxw[:, 2 * hb : 2 * hb + 2],
                in_=tiles["xt%d_%d" % (n, hb)][:].rearrange("q (g u) p -> q g p u", u=2),
            )

        def s1(n):
            qp = getp("qp%d" % n, ps_q, [P, 4, P], "qp")
            for j in range(4):
                for g in range(4):
                    nc.tensor.matmul_mx(
                        out=qp[:, j, :],
                        lhsT=tiles["c_wd%d" % g][:, P * j : P * (j + 1)].bitcast(FP8X4),
                        lhsT_scale=tiles["s_wd%d" % g][:, P * j : P * (j + 1)],
                        rhs=tiles["c_x%d" % n][:, P * g : P * (g + 1)].bitcast(FP8X4),
                        rhs_scale=tiles["s_x%d" % n][:, P * g : P * (g + 1)],
                        start=(g == 0),
                        stop=(g == 3),
                    )

        def q_c(n):
            gq = get("g_q%d" % n, grp, [P, 512], BF16, "gq")
            nc.scalar.copy(
                out=gq[:].rearrange("p (n j) -> p n j", j=4),
                in_=tiles["qp%d" % n][:].rearrange("p j n -> p n j"),
            )

        def s2(kind, pool, n, hg):
            acc = getp("%s%d_%d" % (kind, n, hg), pool, [P, 512], kind)
            nc.tensor.matmul_mx(
                out=acc[:],
                lhsT=tiles["c_q%d" % n][:].bitcast(FP8X4),
                lhsT_scale=tiles["s_q%d" % n][:],
                rhs=tiles["c_%s%d" % (kind, hg)][:].bitcast(FP8X4),
                rhs_scale=tiles["s_%s%d" % (kind, hg)][:],
                start=True,
                stop=True,
            )

        def r_v(n, hg):
            a = get("ab%d_%d" % (n // 2, hg), prod, [P, 2, 2, 512], F32, "ab")
            nc.vector.tensor_tensor(
                out=a[:, n % 2].rearrange("p a (h d) -> p a h d", d=64),
                in0=tiles["rq%d_%d" % (n, hg)][:].rearrange("p (h d) -> p h d", d=64).unsqueeze(1).to_broadcast([P, 2, 8, 64]),
                in1=ct[:, n % 4].unsqueeze(2).to_broadcast([P, 2, 8, 64]),
                op=MULT,
            )

        def n_c(n, hg):
            o = get("ot%d_%d" % (n // 2, hg), res, [P, 8, 2, P], F32, "ot")
            nc.scalar.copy(
                out=o[:, :, n % 2, 64:128],
                in_=tiles["np%d_%d" % (n, hg)][:].rearrange("p (h d) -> p h d", d=64),
            )

        def add(eng, s, hg, half):
            o = get("ot%d_%d" % (s, hg), res, [P, 8, 2, P], F32, "ot")
            a = tiles["ab%d_%d" % (s, hg)]
            lo = 32 * half
            sw = 32 * (1 - half)
            eng.tensor_tensor(
                out=o[:, :, :, lo : lo + 32].rearrange("p h s d -> p s h d"),
                in0=a[:, :, 0].rearrange("p s (h d) -> p s h d", d=64)[:, :, :, lo : lo + 32],
                in1=a[:, :, 1].rearrange("p s (h d) -> p s h d", d=64)[:, :, :, sw : sw + 32],
                op=ADD,
            )

        def store(s, hg):
            b, ip = divmod(s, 2)
            nc.sync.dma_start(
                out=out[b, 8 * hg : 8 * hg + 8].rearrange("h (p i) d -> p h (i d)", i=4)[:, :, 256 * ip : 256 * (ip + 1)],
                in_=tiles["ot%d_%d" % (s, hg)][:].rearrange("p h s d -> p h (s d)"),
            )

        load("x0")
        load("wd0")
        load("wd1")
        load("wd2")
        load("wd3")
        load("x1")
        load("rq0")
        load("x2")
        load("rq1")
        load("x3")
        load("np0")
        load("np1")
        load("x4")
        load("x5")
        load("x6")
        load("x7")
        tables()
        x_t(0, 0)
        x_t(0, 1)
        x_c(0, 0)
        x_c(0, 1)
        regroup("V", "wd0")
        regroup("S", "wd0")
        quantise("x0", 512)
        regroup("V", "wd1")
        regroup("S", "wd1")
        quantise("wd0", 512)
        regroup("V", "wd2")
        regroup("S", "wd2")
        quantise("wd1", 512)
        regroup("V", "wd3")
        regroup("S", "wd3")
        quantise("wd2", 512)
        x_t(1, 0)
        x_t(1, 1)
        x_c(1, 0)
        x_c(1, 1)
        quantise("wd3", 512)
        s1(0)
        quantise("x1", 512)
        regroup("V", "rq0")
        regroup("S", "rq0")
        x_t(2, 0)
        x_t(2, 1)
        q_c(0)
        x_c(2, 0)
        x_c(2, 1)
        s1(1)
        quantise("q0", P)
        regroup("V", "rq1")
        regroup("S", "rq1")
        quantise("rq0", 512)
        quantise("x2", 512)
        x_t(3, 0)
        x_t(3, 1)
        q_c(1)
        x_c(3, 0)
        x_c(3, 1)
        quantise("rq1", 512)
        s1(2)
        s2("rq", ps_r, 0, 0)
        s2("rq", ps_r, 0, 1)
        regroup("V", "np0")
        regroup("S", "np0")
        quantise("x3", 512)
        q_c(2)
        regroup("V", "np1")
        regroup("S", "np1")
        quantise("np0", 512)
        x_t(4, 0)
        x_t(4, 1)
        quantise("np1", 512)
        r_v(0, 0)
        s1(3)
        x_c(4, 0)
        x_c(4, 1)
        quantise("q1", P)
        s2("rq", ps_r, 1, 0)
        s2("rq", ps_r, 1, 1)
        r_v(0, 1)
        q_c(3)
        quantise("x4", 512)
        s2("np", ps_n, 0, 0)
        s2("np", ps_n, 0, 1)
        x_t(5, 0)
        x_t(5, 1)
        r_v(1, 0)
        s1(4)
        n_c(0, 0)
        n_c(0, 1)
        x_c(5, 0)
        x_c(5, 1)
        quantise("q2", P)
        s2("rq", ps_r, 2, 0)
        s2("rq", ps_r, 2, 1)
        r_v(1, 1)
        add(nc.gpsimd, 0, 0, 0)
        add(nc.gpsimd, 0, 0, 1)
        add(nc.gpsimd, 0, 1, 0)
        add(nc.gpsimd, 0, 1, 1)
        q_c(4)
        quantise("x5", 512)
        s2("np", ps_n, 1, 0)
        s2("np", ps_n, 1, 1)
        x_t(6, 0)
        x_t(6, 1)
        r_v(2, 0)
        s1(5)
        n_c(1, 0)
        n_c(1, 1)
        store(0, 0)
        store(0, 1)
        x_c(6, 0)
        x_c(6, 1)
        quantise("q3", P)
        s2("rq", ps_r, 3, 0)
        s2("rq", ps_r, 3, 1)
        r_v(2, 1)
        q_c(5)
        quantise("x6", 512)
        s2("np", ps_n, 2, 0)
        s2("np", ps_n, 2, 1)
        x_t(7, 0)
        x_t(7, 1)
        r_v(3, 0)
        s1(6)
        n_c(2, 0)
        n_c(2, 1)
        x_c(7, 0)
        x_c(7, 1)
        quantise("q4", P)
        s2("rq", ps_r, 4, 0)
        s2("rq", ps_r, 4, 1)
        r_v(3, 1)
        add(nc.gpsimd, 1, 0, 0)
        add(nc.gpsimd, 1, 0, 1)
        add(nc.gpsimd, 1, 1, 0)
        add(nc.gpsimd, 1, 1, 1)
        q_c(6)
        quantise("x7", 512)
        s2("np", ps_n, 3, 0)
        s2("np", ps_n, 3, 1)
        r_v(4, 0)
        s1(7)
        n_c(3, 0)
        n_c(3, 1)
        store(1, 0)
        store(1, 1)
        quantise("q5", P)
        s2("rq", ps_r, 5, 0)
        s2("rq", ps_r, 5, 1)
        r_v(4, 1)
        q_c(7)
        s2("np", ps_n, 4, 0)
        s2("np", ps_n, 4, 1)
        r_v(5, 0)
        n_c(4, 0)
        n_c(4, 1)
        quantise("q6", P)
        s2("rq", ps_r, 6, 0)
        s2("rq", ps_r, 6, 1)
        r_v(5, 1)
        add(nc.gpsimd, 2, 0, 0)
        add(nc.gpsimd, 2, 0, 1)
        add(nc.gpsimd, 2, 1, 0)
        add(nc.gpsimd, 2, 1, 1)
        s2("np", ps_n, 5, 0)
        s2("np", ps_n, 5, 1)
        r_v(6, 0)
        n_c(5, 0)
        n_c(5, 1)
        store(2, 0)
        store(2, 1)
        quantise("q7", P)
        s2("rq", ps_r, 7, 0)
        s2("rq", ps_r, 7, 1)
        r_v(6, 1)
        s2("np", ps_n, 6, 0)
        s2("np", ps_n, 6, 1)
        r_v(7, 0)
        n_c(6, 0)
        n_c(6, 1)
        r_v(7, 1)
        add(nc.vector, 3, 0, 0)
        add(nc.vector, 3, 0, 1)
        add(nc.vector, 3, 1, 0)
        add(nc.vector, 3, 1, 1)
        s2("np", ps_n, 7, 0)
        s2("np", ps_n, 7, 1)
        n_c(7, 0)
        n_c(7, 1)
        store(3, 0)
        store(3, 1)
